import numpy as np
import ml_dtypes

BF16 = ml_dtypes.bfloat16


def bf(x):
    return np.asarray(x, np.float32).astype(BF16)


def f32(x):
    return np.asarray(x, np.float32)


def f64(x):
    return np.asarray(x).astype(np.float64)


def striped(idx):
    return np.tile(idx.reshape(-1, 16).T, (8, 1))


C, S, K, M, H, N = 128, 256, 4, 256, 128, 1024
EPS, SLOPE = 1e-5, 0.2


def setup_inputs():
    return {"x": bf(np.random.standard_normal((C, S))), "w_nbr": bf(np.random.standard_normal((C, M)) / np.sqrt(C)), "w_ctr": bf(np.random.standard_normal((C, M)) / np.sqrt(C)), "gain": f32(1.0 + 0.1 * np.random.standard_normal((M, 1))), "bias": f32(0.1 * np.random.standard_normal((M, 1))), "offs": striped(np.concatenate([np.random.permutation(S)[:H] for _ in range(N // H)]))}


def reference(x, w_nbr, w_ctr, gain, bias, offs):
    idx = offs[:16].T.reshape(-1)
    xs = f64(x)
    ctr = f64(w_ctr).T @ xs - f64(w_nbr).T @ xs
    y = f64(w_nbr).T @ xs[:, idx] + np.tile(ctr, (1, K))
    mean = y.mean(axis=1, keepdims=True)
    var = np.square(y - mean).mean(axis=1, keepdims=True)
    z = (y - mean) / np.sqrt(var + EPS) * f64(gain) + f64(bias)
    return np.maximum(z, SLOPE * z)

@@ -1,0 +1,82 @@
+import concourse.mybir as mybir
+
+BF16, F32, U16 = mybir.dt.bfloat16, mybir.dt.float32, mybir.dt.uint16
+ALU = mybir.AluOpType
+ACT = mybir.ActivationFunctionType
+
+P = 128
+POINTS = 256
+NEIGHBOURS = 4
+EDGES = POINTS * NEIGHBOURS
+FEATURES_OUT = 256
+HALVES = FEATURES_OUT // P
+BLOCKS = HALVES * NEIGHBOURS
+EPS, SLOPE = 1e-5, 0.2
+STATS = 6
+
+FLOPS = 2 * P * FEATURES_OUT * (EDGES + 2 * POINTS)
+
+
+def tile_dgcnn_cls_kernel(tc, x, w_nbr, w_ctr, gain, bias, offs, out):
+    nc = tc.nc
+    with (
+        tc.tile_pool(name="held", bufs=1) as held,
+        tc.tile_pool(name="small", bufs=2) as small,
+        tc.tile_pool(name="work", bufs=BLOCKS) as work,
+        tc.psum_pool(name="psum", bufs=1) as psum,
+    ):
+        points = held.tile([P, POINTS], BF16, name="points")
+        nc.sync.dma_start(points[:], x)
+        offsets = held.tile([P, EDGES // 16], U16, name="offsets")
+        nc.sync.dma_start(offsets[:], offs)
+        ctr_w = held.tile([P, FEATURES_OUT], BF16, name="ctr_w")
+        nc.scalar.dma_start(ctr_w[:], w_ctr)
+        nbr_w = held.tile([P, FEATURES_OUT], BF16, name="nbr_w")
+        nc.scalar.dma_start(nbr_w[:], w_nbr)
+        gain_col = held.tile([P, HALVES], F32, name="gain_col")
+        bias_col = held.tile([P, HALVES], F32, name="bias_col")
+        with nc.allow_non_contiguous_dma(reason="one float32 to a partition, 256 in all"):
+            nc.gpsimd.dma_start(gain_col[:], gain.rearrange("(h p) o -> p (h o)", p=P))
+            nc.gpsimd.dma_start(bias_col[:], bias.rearrange("(h p) o -> p (h o)", p=P))
+
+        neg_nbr_w = held.tile([P, FEATURES_OUT], BF16, name="neg_nbr_w")
+        nc.vector.tensor_scalar_mul(neg_nbr_w[:], nbr_w[:], -1.0)
+        signed_gain = held.tile([P, HALVES, 2], F32, name="signed_gain")
+        nc.vector.tensor_copy(signed_gain[:, :, 0], gain_col[:])
+        nc.vector.tensor_scalar_mul(signed_gain[:, :, 1], gain_col[:], -1.0)
+        eps_col = held.tile([P, 1], F32, name="eps_col")
+        nc.vector.memset(eps_col[:], EPS)
+
+        halves = [slice(h * P, (h + 1) * P) for h in range(HALVES)]
+        y = [[psum.tile([P, POINTS], F32, name=f"y{h}_{r}") for r in range(NEIGHBOURS)] for h in range(HALVES)]
+        for h in range(HALVES):
+            for r in range(NEIGHBOURS):
+                nc.tensor.matmul(y[h][r][:], ctr_w[:, halves[h]], points[:], start=True, stop=False)
+            for r in range(NEIGHBOURS):
+                nc.tensor.matmul(y[h][r][:], neg_nbr_w[:, halves[h]], points[:], start=False, stop=False)
+
+        stats = [small.tile([P, NEIGHBOURS, STATS], F32, name=f"stats{h}") for h in range(HALVES)]
+        for h in range(HALVES):
+            for r in range(NEIGHBOURS):
+                piece = offsets[:, r * (POINTS // 16) : (r + 1) * (POINTS // 16)]
+                nc.tensor.matmul(y[h][r][:], nbr_w[:, halves[h]], points[:].indirect(piece), start=False, stop=True)
+                nc.vector.bn_stats(stats[h][:, r, :], y[h][r][:])
+
+        for h in range(HALVES):
+            mean_var = small.tile([P, 2], F32, name="mean_var")
+            nc.vector.bn_aggr(mean_var[:], stats[h][:].rearrange("p r s -> p (r s)"))
+            rstd = small.tile([P, 1], F32, name="rstd")
+            nc.scalar.activation(rstd[:], mean_var[:, 1:2], ACT.Abs_reciprocal_sqrt, bias=eps_col[:], scale=1.0)
+            signed_scale = small.tile([P, 2], F32, name="signed_scale")
+            nc.vector.tensor_scalar_mul(signed_scale[:], signed_gain[:, h, :], rstd[:])
+            shift = small.tile([P, 1], F32, name="shift")
+            nc.vector.tensor_scalar(
+                shift[:], mean_var[:, 0:1], signed_scale[:, 1:2], bias_col[:, h : h + 1], ALU.mult, ALU.add
+            )
+
+            for r in range(NEIGHBOURS):
+                z = work.tile([P, POINTS], F32, name="z")
+                nc.scalar.activation(z[:], y[h][r][:], ACT.Identity, bias=shift[:], scale=signed_scale[:, 0:1])
+                result = work.tile([P, POINTS], F32, name="result")
+                nc.vector.scalar_tensor_tensor(result[:], z[:], SLOPE, z[:], ALU.mult, ALU.max)
+                nc.sync.dma_start(out[halves[h], r * POINTS : (r + 1) * POINTS], result[:])

@@ -21,18 +21,18 @@ def tile_dgcnn_cls_kernel(tc, x, w_nbr, w_ctr, gain, bias, offs, out):
     nc = tc.nc
     with (
         tc.tile_pool(name="held", bufs=1) as held,
-        tc.tile_pool(name="small", bufs=2) as small,
+        tc.tile_pool(name="small", bufs=HALVES) as small,
         tc.tile_pool(name="work", bufs=BLOCKS) as work,
         tc.psum_pool(name="psum", bufs=1) as psum,
     ):
+        nbr_w = held.tile([P, FEATURES_OUT], BF16, name="nbr_w")
+        nc.sync.dma_start(nbr_w[:], w_nbr)
         points = held.tile([P, POINTS], BF16, name="points")
-        nc.sync.dma_start(points[:], x)
-        offsets = held.tile([P, EDGES // 16], U16, name="offsets")
-        nc.sync.dma_start(offsets[:], offs)
+        nc.scalar.dma_start(points[:], x)
         ctr_w = held.tile([P, FEATURES_OUT], BF16, name="ctr_w")
         nc.scalar.dma_start(ctr_w[:], w_ctr)
-        nbr_w = held.tile([P, FEATURES_OUT], BF16, name="nbr_w")
-        nc.scalar.dma_start(nbr_w[:], w_nbr)
+        offsets = held.tile([P, EDGES // 16], U16, name="offsets")
+        nc.sync.dma_start(offsets[:], offs)
         gain_col = held.tile([P, HALVES], F32, name="gain_col")
         bias_col = held.tile([P, HALVES], F32, name="bias_col")
         with nc.allow_non_contiguous_dma(reason="one float32 to a partition, 256 in all"):
@@ -41,42 +41,48 @@ def tile_dgcnn_cls_kernel(tc, x, w_nbr, w_ctr, gain, bias, offs, out):
 
         neg_nbr_w = held.tile([P, FEATURES_OUT], BF16, name="neg_nbr_w")
         nc.vector.tensor_scalar_mul(neg_nbr_w[:], nbr_w[:], -1.0)
-        signed_gain = held.tile([P, HALVES, 2], F32, name="signed_gain")
-        nc.vector.tensor_copy(signed_gain[:, :, 0], gain_col[:])
-        nc.vector.tensor_scalar_mul(signed_gain[:, :, 1], gain_col[:], -1.0)
+        neg_gain_col = held.tile([P, HALVES], F32, name="neg_gain_col")
+        nc.vector.tensor_scalar_mul(neg_gain_col[:], gain_col[:], -1.0)
         eps_col = held.tile([P, 1], F32, name="eps_col")
         nc.vector.memset(eps_col[:], EPS)
 
         halves = [slice(h * P, (h + 1) * P) for h in range(HALVES)]
+        pieces = [offsets[:, r * (POINTS // 16) : (r + 1) * (POINTS // 16)] for r in range(NEIGHBOURS)]
         y = [[psum.tile([P, POINTS], F32, name=f"y{h}_{r}") for r in range(NEIGHBOURS)] for h in range(HALVES)]
-        for h in range(HALVES):
-            for r in range(NEIGHBOURS):
-                nc.tensor.matmul(y[h][r][:], ctr_w[:, halves[h]], points[:], start=True, stop=False)
-            for r in range(NEIGHBOURS):
-                nc.tensor.matmul(y[h][r][:], neg_nbr_w[:, halves[h]], points[:], start=False, stop=False)
+        for r in range(NEIGHBOURS):
+            nc.tensor.matmul(y[0][r][:], ctr_w[:, halves[0]], points[:], start=True, stop=False)
+        for r in range(NEIGHBOURS):
+            nc.tensor.matmul(y[0][r][:], neg_nbr_w[:, halves[0]], points[:], start=False, stop=False)
+        for r in range(NEIGHBOURS):
+            nc.tensor.matmul(y[0][r][:], nbr_w[:, halves[0]], points[:].indirect(pieces[r]), start=False, stop=True)
+        for r in range(NEIGHBOURS):
+            nc.tensor.matmul(y[1][r][:], nbr_w[:, halves[1]], points[:].indirect(pieces[r]), start=True, stop=False)
+        for r in range(NEIGHBOURS):
+            nc.tensor.matmul(y[1][r][:], ctr_w[:, halves[1]], points[:], start=False, stop=False)
+            nc.tensor.matmul(y[1][r][:], neg_nbr_w[:, halves[1]], points[:], start=False, stop=True)
 
-        stats = [small.tile([P, NEIGHBOURS, STATS], F32, name=f"stats{h}") for h in range(HALVES)]
+        z = [[work.tile([P, POINTS], F32, name="z") for r in range(NEIGHBOURS)] for h in range(HALVES)]
         for h in range(HALVES):
+            stats = small.tile([P, NEIGHBOURS, STATS], F32, name="stats")
             for r in range(NEIGHBOURS):
-                piece = offsets[:, r * (POINTS // 16) : (r + 1) * (POINTS // 16)]
-                nc.tensor.matmul(y[h][r][:], nbr_w[:, halves[h]], points[:].indirect(piece), start=False, stop=True)
-                nc.vector.bn_stats(stats[h][:, r, :], y[h][r][:])
-
-        for h in range(HALVES):
+                nc.vector.bn_stats(stats[:, r, :], y[h][r][:])
             mean_var = small.tile([P, 2], F32, name="mean_var")
-            nc.vector.bn_aggr(mean_var[:], stats[h][:].rearrange("p r s -> p (r s)"))
+            nc.vector.bn_aggr(mean_var[:], stats[:].rearrange("p r s -> p (r s)"))
             rstd = small.tile([P, 1], F32, name="rstd")
             nc.scalar.activation(rstd[:], mean_var[:, 1:2], ACT.Abs_reciprocal_sqrt, bias=eps_col[:], scale=1.0)
-            signed_scale = small.tile([P, 2], F32, name="signed_scale")
-            nc.vector.tensor_scalar_mul(signed_scale[:], signed_gain[:, h, :], rstd[:])
+            scale = small.tile([P, 1], F32, name="scale")
+            nc.scalar.activation(scale[:], rstd[:], ACT.Identity, scale=gain_col[:, h : h + 1])
+            neg_scale = small.tile([P, 1], F32, name="neg_scale")
+            nc.scalar.activation(neg_scale[:], rstd[:], ACT.Identity, scale=neg_gain_col[:, h : h + 1])
             shift = small.tile([P, 1], F32, name="shift")
-            nc.vector.tensor_scalar(
-                shift[:], mean_var[:, 0:1], signed_scale[:, 1:2], bias_col[:, h : h + 1], ALU.mult, ALU.add
+            nc.scalar.activation(
+                shift[:], mean_var[:, 0:1], ACT.Identity, bias=bias_col[:, h : h + 1], scale=neg_scale[:]
             )
-
             for r in range(NEIGHBOURS):
-                z = work.tile([P, POINTS], F32, name="z")
-                nc.scalar.activation(z[:], y[h][r][:], ACT.Identity, bias=shift[:], scale=signed_scale[:, 0:1])
+                nc.scalar.activation(z[h][r][:], y[h][r][:], ACT.Identity, bias=shift[:], scale=scale[:])
+
+        for h in range(HALVES):
+            for r in range(NEIGHBOURS):
                 result = work.tile([P, POINTS], F32, name="result")
-                nc.vector.scalar_tensor_tensor(result[:], z[:], SLOPE, z[:], ALU.mult, ALU.max)
+                nc.vector.scalar_tensor_tensor(result[:], z[h][r][:], SLOPE, z[h][r][:], ALU.mult, ALU.max)
                 nc.sync.dma_start(out[halves[h], r * POINTS : (r + 1) * POINTS], result[:])

@@ -36,8 +36,8 @@ def tile_dgcnn_cls_kernel(tc, x, w_nbr, w_ctr, gain, bias, offs, out):
         gain_col = held.tile([P, HALVES], F32, name="gain_col")
         bias_col = held.tile([P, HALVES], F32, name="bias_col")
         with nc.allow_non_contiguous_dma(reason="one float32 to a partition, 256 in all"):
-            nc.gpsimd.dma_start(gain_col[:], gain.rearrange("(h p) o -> p (h o)", p=P))
-            nc.gpsimd.dma_start(bias_col[:], bias.rearrange("(h p) o -> p (h o)", p=P))
+            nc.sync.dma_start(gain_col[:], gain.rearrange("(h p) o -> p (h o)", p=P))
+            nc.scalar.dma_start(bias_col[:], bias.rearrange("(h p) o -> p (h o)", p=P))
 
         neg_nbr_w = held.tile([P, FEATURES_OUT], BF16, name="neg_nbr_w")
         nc.vector.tensor_scalar_mul(neg_nbr_w[:], nbr_w[:], -1.0)

@@ -45,21 +45,23 @@ def tile_dgcnn_cls_kernel(tc, x, w_nbr, w_ctr, gain, bias, offs, out):
         nc.vector.tensor_scalar_mul(neg_gain_col[:], gain_col[:], -1.0)
         eps_col = held.tile([P, 1], F32, name="eps_col")
         nc.vector.memset(eps_col[:], EPS)
+        table_warmer = held.tile([P, 1], F32, name="table_warmer")
+        nc.scalar.activation(table_warmer[:], eps_col[:], ACT.Abs_reciprocal_sqrt)
 
         halves = [slice(h * P, (h + 1) * P) for h in range(HALVES)]
         pieces = [offsets[:, r * (POINTS // 16) : (r + 1) * (POINTS // 16)] for r in range(NEIGHBOURS)]
         y = [[psum.tile([P, POINTS], F32, name=f"y{h}_{r}") for r in range(NEIGHBOURS)] for h in range(HALVES)]
-        for r in range(NEIGHBOURS):
-            nc.tensor.matmul(y[0][r][:], ctr_w[:, halves[0]], points[:], start=True, stop=False)
-        for r in range(NEIGHBOURS):
-            nc.tensor.matmul(y[0][r][:], neg_nbr_w[:, halves[0]], points[:], start=False, stop=False)
-        for r in range(NEIGHBOURS):
-            nc.tensor.matmul(y[0][r][:], nbr_w[:, halves[0]], points[:].indirect(pieces[r]), start=False, stop=True)
-        for r in range(NEIGHBOURS):
-            nc.tensor.matmul(y[1][r][:], nbr_w[:, halves[1]], points[:].indirect(pieces[r]), start=True, stop=False)
-        for r in range(NEIGHBOURS):
-            nc.tensor.matmul(y[1][r][:], ctr_w[:, halves[1]], points[:], start=False, stop=False)
-            nc.tensor.matmul(y[1][r][:], neg_nbr_w[:, halves[1]], points[:], start=False, stop=True)
+        for h in range(HALVES):
+            for r in range(NEIGHBOURS):
+                nc.tensor.matmul(y[h][r][:], ctr_w[:, halves[h]], points[:], start=True, stop=False)
+        for h in range(HALVES):
+            for r in range(NEIGHBOURS):
+                nc.tensor.matmul(y[h][r][:], neg_nbr_w[:, halves[h]], points[:], start=False, stop=False)
+        for h in range(HALVES):
+            for r in range(NEIGHBOURS):
+                nc.tensor.matmul(
+                    y[h][r][:], nbr_w[:, halves[h]], points[:].indirect(pieces[r]), start=False, stop=True
+                )
 
         z = [[work.tile([P, POINTS], F32, name="z") for r in range(NEIGHBOURS)] for h in range(HALVES)]
         for h in range(HALVES):
@@ -70,14 +72,12 @@ def tile_dgcnn_cls_kernel(tc, x, w_nbr, w_ctr, gain, bias, offs, out):
             nc.vector.bn_aggr(mean_var[:], stats[:].rearrange("p r s -> p (r s)"))
             rstd = small.tile([P, 1], F32, name="rstd")
             nc.scalar.activation(rstd[:], mean_var[:, 1:2], ACT.Abs_reciprocal_sqrt, bias=eps_col[:], scale=1.0)
+            neg_mean_gain = small.tile([P, 1], F32, name="neg_mean_gain")
+            nc.vector.tensor_mul(neg_mean_gain[:], mean_var[:, 0:1], neg_gain_col[:, h : h + 1])
             scale = small.tile([P, 1], F32, name="scale")
             nc.scalar.activation(scale[:], rstd[:], ACT.Identity, scale=gain_col[:, h : h + 1])
-            neg_scale = small.tile([P, 1], F32, name="neg_scale")
-            nc.scalar.activation(neg_scale[:], rstd[:], ACT.Identity, scale=neg_gain_col[:, h : h + 1])
             shift = small.tile([P, 1], F32, name="shift")
-            nc.scalar.activation(
-                shift[:], mean_var[:, 0:1], ACT.Identity, bias=bias_col[:, h : h + 1], scale=neg_scale[:]
-            )
+            nc.scalar.activation(shift[:], rstd[:], ACT.Identity, bias=bias_col[:, h : h + 1], scale=neg_mean_gain[:])
             for r in range(NEIGHBOURS):
                 nc.scalar.activation(z[h][r][:], y[h][r][:], ACT.Identity, bias=shift[:], scale=scale[:])
 

@@ -13,6 +13,7 @@ HALVES = FEATURES_OUT // P
 BLOCKS = HALVES * NEIGHBOURS
 EPS, SLOPE = 1e-5, 0.2
 STATS = 6
+WARM_MATMULS = 8
 
 FLOPS = 2 * P * FEATURES_OUT * (EDGES + 2 * POINTS)
 
@@ -51,6 +52,10 @@ def tile_dgcnn_cls_kernel(tc, x, w_nbr, w_ctr, gain, bias, offs, out):
         halves = [slice(h * P, (h + 1) * P) for h in range(HALVES)]
         pieces = [offsets[:, r * (POINTS // 16) : (r + 1) * (POINTS // 16)] for r in range(NEIGHBOURS)]
         y = [[psum.tile([P, POINTS], F32, name=f"y{h}_{r}") for r in range(NEIGHBOURS)] for h in range(HALVES)]
+        zeros = held.tile([P, POINTS], BF16, name="zeros")
+        nc.gpsimd.memset(zeros[:], 0.0)
+        for i in range(WARM_MATMULS):
+            nc.tensor.matmul(y[HALVES - 1][NEIGHBOURS - 1][:], zeros[:, 0:P], zeros[:], start=True, stop=True)
         for h in range(HALVES):
             for r in range(NEIGHBOURS):
                 nc.tensor.matmul(y[h][r][:], ctr_w[:, halves[h]], points[:], start=True, stop=False)

@@ -26,6 +26,9 @@ def tile_dgcnn_cls_kernel(tc, x, w_nbr, w_ctr, gain, bias, offs, out):
         tc.tile_pool(name="work", bufs=BLOCKS) as work,
         tc.psum_pool(name="psum", bufs=1) as psum,
     ):
+        zeros = held.tile([P, POINTS], BF16, name="zeros")
+        nc.vector.memset(zeros[:], 0.0)
+
         nbr_w = held.tile([P, FEATURES_OUT], BF16, name="nbr_w")
         nc.sync.dma_start(nbr_w[:], w_nbr)
         points = held.tile([P, POINTS], BF16, name="points")
@@ -52,21 +55,19 @@ def tile_dgcnn_cls_kernel(tc, x, w_nbr, w_ctr, gain, bias, offs, out):
         halves = [slice(h * P, (h + 1) * P) for h in range(HALVES)]
         pieces = [offsets[:, r * (POINTS // 16) : (r + 1) * (POINTS // 16)] for r in range(NEIGHBOURS)]
         y = [[psum.tile([P, POINTS], F32, name=f"y{h}_{r}") for r in range(NEIGHBOURS)] for h in range(HALVES)]
-        zeros = held.tile([P, POINTS], BF16, name="zeros")
-        nc.gpsimd.memset(zeros[:], 0.0)
         for i in range(WARM_MATMULS):
             nc.tensor.matmul(y[HALVES - 1][NEIGHBOURS - 1][:], zeros[:, 0:P], zeros[:], start=True, stop=True)
-        for h in range(HALVES):
-            for r in range(NEIGHBOURS):
-                nc.tensor.matmul(y[h][r][:], ctr_w[:, halves[h]], points[:], start=True, stop=False)
-        for h in range(HALVES):
-            for r in range(NEIGHBOURS):
-                nc.tensor.matmul(y[h][r][:], neg_nbr_w[:, halves[h]], points[:], start=False, stop=False)
-        for h in range(HALVES):
-            for r in range(NEIGHBOURS):
-                nc.tensor.matmul(
-                    y[h][r][:], nbr_w[:, halves[h]], points[:].indirect(pieces[r]), start=False, stop=True
-                )
+        for r in range(NEIGHBOURS):
+            nc.tensor.matmul(y[0][r][:], ctr_w[:, halves[0]], points[:], start=True, stop=False)
+        for r in range(NEIGHBOURS):
+            nc.tensor.matmul(y[0][r][:], neg_nbr_w[:, halves[0]], points[:], start=False, stop=False)
+        for r in range(NEIGHBOURS):
+            nc.tensor.matmul(y[0][r][:], nbr_w[:, halves[0]], points[:].indirect(pieces[r]), start=False, stop=True)
+        for r in range(NEIGHBOURS):
+            nc.tensor.matmul(y[1][r][:], nbr_w[:, halves[1]], points[:].indirect(pieces[r]), start=True, stop=False)
+        for r in range(NEIGHBOURS):
+            nc.tensor.matmul(y[1][r][:], ctr_w[:, halves[1]], points[:], start=False, stop=False)
+            nc.tensor.matmul(y[1][r][:], neg_nbr_w[:, halves[1]], points[:], start=False, stop=True)
 
         z = [[work.tile([P, POINTS], F32, name="z") for r in range(NEIGHBOURS)] for h in range(HALVES)]
         for h in range(HALVES):

@@ -29,12 +29,12 @@ def tile_dgcnn_cls_kernel(tc, x, w_nbr, w_ctr, gain, bias, offs, out):
         zeros = held.tile([P, POINTS], BF16, name="zeros")
         nc.vector.memset(zeros[:], 0.0)
 
-        nbr_w = held.tile([P, FEATURES_OUT], BF16, name="nbr_w")
-        nc.sync.dma_start(nbr_w[:], w_nbr)
         points = held.tile([P, POINTS], BF16, name="points")
-        nc.scalar.dma_start(points[:], x)
+        nc.sync.dma_start(points[:], x)
         ctr_w = held.tile([P, FEATURES_OUT], BF16, name="ctr_w")
         nc.scalar.dma_start(ctr_w[:], w_ctr)
+        nbr_w = held.tile([P, FEATURES_OUT], BF16, name="nbr_w")
+        nc.scalar.dma_start(nbr_w[:], w_nbr)
         offsets = held.tile([P, EDGES // 16], U16, name="offsets")
         nc.sync.dma_start(offsets[:], offs)
         gain_col = held.tile([P, HALVES], F32, name="gain_col")
@@ -43,8 +43,8 @@ def tile_dgcnn_cls_kernel(tc, x, w_nbr, w_ctr, gain, bias, offs, out):
             nc.sync.dma_start(gain_col[:], gain.rearrange("(h p) o -> p (h o)", p=P))
             nc.scalar.dma_start(bias_col[:], bias.rearrange("(h p) o -> p (h o)", p=P))
 
-        neg_nbr_w = held.tile([P, FEATURES_OUT], BF16, name="neg_nbr_w")
-        nc.vector.tensor_scalar_mul(neg_nbr_w[:], nbr_w[:], -1.0)
+        neg_points = held.tile([P, POINTS], BF16, name="neg_points")
+        nc.vector.tensor_scalar_mul(neg_points[:], points[:], -1.0)
         neg_gain_col = held.tile([P, HALVES], F32, name="neg_gain_col")
         nc.vector.tensor_scalar_mul(neg_gain_col[:], gain_col[:], -1.0)
         eps_col = held.tile([P, 1], F32, name="eps_col")
@@ -60,14 +60,14 @@ def tile_dgcnn_cls_kernel(tc, x, w_nbr, w_ctr, gain, bias, offs, out):
         for r in range(NEIGHBOURS):
             nc.tensor.matmul(y[0][r][:], ctr_w[:, halves[0]], points[:], start=True, stop=False)
         for r in range(NEIGHBOURS):
-            nc.tensor.matmul(y[0][r][:], neg_nbr_w[:, halves[0]], points[:], start=False, stop=False)
+            nc.tensor.matmul(y[0][r][:], nbr_w[:, halves[0]], neg_points[:], start=False, stop=False)
         for r in range(NEIGHBOURS):
             nc.tensor.matmul(y[0][r][:], nbr_w[:, halves[0]], points[:].indirect(pieces[r]), start=False, stop=True)
         for r in range(NEIGHBOURS):
             nc.tensor.matmul(y[1][r][:], nbr_w[:, halves[1]], points[:].indirect(pieces[r]), start=True, stop=False)
         for r in range(NEIGHBOURS):
             nc.tensor.matmul(y[1][r][:], ctr_w[:, halves[1]], points[:], start=False, stop=False)
-            nc.tensor.matmul(y[1][r][:], neg_nbr_w[:, halves[1]], points[:], start=False, stop=True)
+            nc.tensor.matmul(y[1][r][:], nbr_w[:, halves[1]], neg_points[:], start=False, stop=True)
 
         z = [[work.tile([P, POINTS], F32, name="z") for r in range(NEIGHBOURS)] for h in range(HALVES)]
         for h in range(HALVES):

@@ -13,7 +13,7 @@ HALVES = FEATURES_OUT // P
 BLOCKS = HALVES * NEIGHBOURS
 EPS, SLOPE = 1e-5, 0.2
 STATS = 6
-WARM_MATMULS = 8
+WARM_MATMULS = 6
 
 FLOPS = 2 * P * FEATURES_OUT * (EDGES + 2 * POINTS)
 

@@ -79,7 +79,7 @@ def tile_dgcnn_cls_kernel(tc, x, w_nbr, w_ctr, gain, bias, offs, out):
             rstd = small.tile([P, 1], F32, name="rstd")
             nc.scalar.activation(rstd[:], mean_var[:, 1:2], ACT.Abs_reciprocal_sqrt, bias=eps_col[:], scale=1.0)
             neg_mean_gain = small.tile([P, 1], F32, name="neg_mean_gain")
-            nc.vector.tensor_mul(neg_mean_gain[:], mean_var[:, 0:1], neg_gain_col[:, h : h + 1])
+            nc.scalar.activation(neg_mean_gain[:], mean_var[:, 0:1], ACT.Identity, scale=neg_gain_col[:, h : h + 1])
             scale = small.tile([P, 1], F32, name="scale")
             nc.scalar.activation(scale[:], rstd[:], ACT.Identity, scale=gain_col[:, h : h + 1])
             shift = small.tile([P, 1], F32, name="shift")

@@ -30,13 +30,13 @@ def tile_dgcnn_cls_kernel(tc, x, w_nbr, w_ctr, gain, bias, offs, out):
         nc.vector.memset(zeros[:], 0.0)
 
         points = held.tile([P, POINTS], BF16, name="points")
-        nc.sync.dma_start(points[:], x)
-        ctr_w = held.tile([P, FEATURES_OUT], BF16, name="ctr_w")
-        nc.scalar.dma_start(ctr_w[:], w_ctr)
-        nbr_w = held.tile([P, FEATURES_OUT], BF16, name="nbr_w")
-        nc.scalar.dma_start(nbr_w[:], w_nbr)
+        nc.scalar.dma_start(points[:], x)
         offsets = held.tile([P, EDGES // 16], U16, name="offsets")
         nc.sync.dma_start(offsets[:], offs)
+        nbr_w = held.tile([P, FEATURES_OUT], BF16, name="nbr_w")
+        nc.sync.dma_start(nbr_w[:], w_nbr)
+        ctr_w = held.tile([P, FEATURES_OUT], BF16, name="ctr_w")
+        nc.scalar.dma_start(ctr_w[:], w_ctr)
         gain_col = held.tile([P, HALVES], F32, name="gain_col")
         bias_col = held.tile([P, HALVES], F32, name="bias_col")
         with nc.allow_non_contiguous_dma(reason="one float32 to a partition, 256 in all"):
@@ -52,22 +52,26 @@ def tile_dgcnn_cls_kernel(tc, x, w_nbr, w_ctr, gain, bias, offs, out):
         table_warmer = held.tile([P, 1], F32, name="table_warmer")
         nc.scalar.activation(table_warmer[:], eps_col[:], ACT.Abs_reciprocal_sqrt)
 
+        point_parts = [slice(0, POINTS // 2), slice(POINTS // 2, POINTS)]
         halves = [slice(h * P, (h + 1) * P) for h in range(HALVES)]
         pieces = [offsets[:, r * (POINTS // 16) : (r + 1) * (POINTS // 16)] for r in range(NEIGHBOURS)]
         y = [[psum.tile([P, POINTS], F32, name=f"y{h}_{r}") for r in range(NEIGHBOURS)] for h in range(HALVES)]
         for i in range(WARM_MATMULS):
             nc.tensor.matmul(y[HALVES - 1][NEIGHBOURS - 1][:], zeros[:, 0:P], zeros[:], start=True, stop=True)
         for r in range(NEIGHBOURS):
-            nc.tensor.matmul(y[0][r][:], ctr_w[:, halves[0]], points[:], start=True, stop=False)
+            nc.tensor.matmul(y[0][r][:], nbr_w[:, halves[0]], points[:].indirect(pieces[r]), start=True, stop=False)
         for r in range(NEIGHBOURS):
-            nc.tensor.matmul(y[0][r][:], nbr_w[:, halves[0]], neg_points[:], start=False, stop=False)
+            for t in point_parts:
+                nc.tensor.matmul(y[0][r][:, t], ctr_w[:, halves[0]], points[:, t], start=False, stop=False)
+            for t in point_parts:
+                nc.tensor.matmul(
+                    y[0][r][:, t], nbr_w[:, halves[0]], neg_points[:, t], start=False, stop=t == point_parts[-1]
+                )
         for r in range(NEIGHBOURS):
-            nc.tensor.matmul(y[0][r][:], nbr_w[:, halves[0]], points[:].indirect(pieces[r]), start=False, stop=True)
+            nc.tensor.matmul(y[1][r][:], ctr_w[:, halves[1]], points[:], start=True, stop=False)
+            nc.tensor.matmul(y[1][r][:], nbr_w[:, halves[1]], neg_points[:], start=False, stop=False)
         for r in range(NEIGHBOURS):
-            nc.tensor.matmul(y[1][r][:], nbr_w[:, halves[1]], points[:].indirect(pieces[r]), start=True, stop=False)
-        for r in range(NEIGHBOURS):
-            nc.tensor.matmul(y[1][r][:], ctr_w[:, halves[1]], points[:], start=False, stop=False)
-            nc.tensor.matmul(y[1][r][:], nbr_w[:, halves[1]], neg_points[:], start=False, stop=True)
+            nc.tensor.matmul(y[1][r][:], nbr_w[:, halves[1]], points[:].indirect(pieces[r]), start=False, stop=True)
 
         z = [[work.tile([P, POINTS], F32, name="z") for r in range(NEIGHBOURS)] for h in range(HALVES)]
         for h in range(HALVES):

@@ -61,15 +61,13 @@ def tile_dgcnn_cls_kernel(tc, x, w_nbr, w_ctr, gain, bias, offs, out):
         for r in range(NEIGHBOURS):
             nc.tensor.matmul(y[0][r][:], nbr_w[:, halves[0]], points[:].indirect(pieces[r]), start=True, stop=False)
         for r in range(NEIGHBOURS):
-            for t in point_parts:
-                nc.tensor.matmul(y[0][r][:, t], ctr_w[:, halves[0]], points[:, t], start=False, stop=False)
-            for t in point_parts:
-                nc.tensor.matmul(
-                    y[0][r][:, t], nbr_w[:, halves[0]], neg_points[:, t], start=False, stop=t == point_parts[-1]
-                )
+            nc.tensor.matmul(y[0][r][:], ctr_w[:, halves[0]], points[:], start=False, stop=False)
+            nc.tensor.matmul(y[0][r][:], nbr_w[:, halves[0]], neg_points[:], start=False, stop=True)
         for r in range(NEIGHBOURS):
-            nc.tensor.matmul(y[1][r][:], ctr_w[:, halves[1]], points[:], start=True, stop=False)
-            nc.tensor.matmul(y[1][r][:], nbr_w[:, halves[1]], neg_points[:], start=False, stop=False)
+            for i, t in enumerate(point_parts):
+                nc.tensor.matmul(y[1][r][:, t], ctr_w[:, halves[1]], points[:, t], start=i == 0, stop=False)
+            for t in point_parts:
+                nc.tensor.matmul(y[1][r][:, t], nbr_w[:, halves[1]], neg_points[:, t], start=False, stop=False)
         for r in range(NEIGHBOURS):
             nc.tensor.matmul(y[1][r][:], nbr_w[:, halves[1]], points[:].indirect(pieces[r]), start=False, stop=True)
 

@@ -29,12 +29,12 @@ def tile_dgcnn_cls_kernel(tc, x, w_nbr, w_ctr, gain, bias, offs, out):
         zeros = held.tile([P, POINTS], BF16, name="zeros")
         nc.vector.memset(zeros[:], 0.0)
 
+        nbr_w = held.tile([P, FEATURES_OUT], BF16, name="nbr_w")
+        nc.sync.dma_start(nbr_w[:], w_nbr)
         points = held.tile([P, POINTS], BF16, name="points")
         nc.scalar.dma_start(points[:], x)
         offsets = held.tile([P, EDGES // 16], U16, name="offsets")
         nc.sync.dma_start(offsets[:], offs)
-        nbr_w = held.tile([P, FEATURES_OUT], BF16, name="nbr_w")
-        nc.sync.dma_start(nbr_w[:], w_nbr)
         ctr_w = held.tile([P, FEATURES_OUT], BF16, name="ctr_w")
         nc.scalar.dma_start(ctr_w[:], w_ctr)
         gain_col = held.tile([P, HALVES], F32, name="gain_col")
@@ -72,6 +72,10 @@ def tile_dgcnn_cls_kernel(tc, x, w_nbr, w_ctr, gain, bias, offs, out):
             nc.tensor.matmul(y[1][r][:], nbr_w[:, halves[1]], points[:].indirect(pieces[r]), start=False, stop=True)
 
         z = [[work.tile([P, POINTS], F32, name="z") for r in range(NEIGHBOURS)] for h in range(HALVES)]
+
+        def parts(h, r):
+            return point_parts if (h, r) == (HALVES - 1, NEIGHBOURS - 1) else [slice(0, POINTS)]
+
         for h in range(HALVES):
             stats = small.tile([P, NEIGHBOURS, STATS], F32, name="stats")
             for r in range(NEIGHBOURS):
@@ -87,10 +91,22 @@ def tile_dgcnn_cls_kernel(tc, x, w_nbr, w_ctr, gain, bias, offs, out):
             shift = small.tile([P, 1], F32, name="shift")
             nc.scalar.activation(shift[:], rstd[:], ACT.Identity, bias=bias_col[:, h : h + 1], scale=neg_mean_gain[:])
             for r in range(NEIGHBOURS):
-                nc.scalar.activation(z[h][r][:], y[h][r][:], ACT.Identity, bias=shift[:], scale=scale[:])
+                if h == HALVES - 1 and r == 0:
+                    centred = work.tile([P, POINTS], F32, name="centred")
+                    nc.vector.tensor_scalar(
+                        centred[:], y[h][r][:], mean_var[:, 0:1], gain_col[:, h : h + 1], ALU.subtract, ALU.mult
+                    )
+                    nc.scalar.activation(
+                        z[h][r][:], centred[:], ACT.Identity, bias=bias_col[:, h : h + 1], scale=rstd[:]
+                    )
+                else:
+                    for t in parts(h, r):
+                        nc.scalar.activation(z[h][r][:, t], y[h][r][:, t], ACT.Identity, bias=shift[:], scale=scale[:])
 
         for h in range(HALVES):
             for r in range(NEIGHBOURS):
-                result = work.tile([P, POINTS], F32, name="result")
-                nc.vector.scalar_tensor_tensor(result[:], z[h][r][:], SLOPE, z[h][r][:], ALU.mult, ALU.max)
-                nc.sync.dma_start(out[halves[h], r * POINTS : (r + 1) * POINTS], result[:])
+                for t in parts(h, r):
+                    z_part = z[h][r][:, t]
+                    result = work.tile([P, t.stop - t.start], F32, name=f"result{t.start}_{t.stop}")
+                    nc.vector.scalar_tensor_tensor(result[:], z_part, SLOPE, z_part, ALU.mult, ALU.max)
+                    nc.sync.dma_start(out[halves[h], r * POINTS + t.start : r * POINTS + t.stop], result[:])

import concourse.mybir as mybir

BF16, F32, U16 = mybir.dt.bfloat16, mybir.dt.float32, mybir.dt.uint16
ALU = mybir.AluOpType
ACT = mybir.ActivationFunctionType

P = 128
POINTS = 256
NEIGHBOURS = 4
EDGES = POINTS * NEIGHBOURS
FEATURES_OUT = 256
HALVES = FEATURES_OUT // P
BLOCKS = HALVES * NEIGHBOURS
EPS, SLOPE = 1e-5, 0.2
STATS = 6
WARM_MATMULS = 6

FLOPS = 2 * P * FEATURES_OUT * (EDGES + 2 * POINTS)


def tile_dgcnn_cls_kernel(tc, x, w_nbr, w_ctr, gain, bias, offs, out):
    nc = tc.nc
    with (
        tc.tile_pool(name="held", bufs=1) as held,
        tc.tile_pool(name="small", bufs=HALVES) as small,
        tc.tile_pool(name="work", bufs=BLOCKS) as work,
        tc.psum_pool(name="psum", bufs=1) as psum,
    ):
        zeros = held.tile([P, POINTS], BF16, name="zeros")
        nc.vector.memset(zeros[:], 0.0)

        nbr_w = held.tile([P, FEATURES_OUT], BF16, name="nbr_w")
        nc.sync.dma_start(nbr_w[:], w_nbr)
        points = held.tile([P, POINTS], BF16, name="points")
        nc.scalar.dma_start(points[:], x)
        offsets = held.tile([P, EDGES // 16], U16, name="offsets")
        nc.sync.dma_start(offsets[:], offs)
        ctr_w = held.tile([P, FEATURES_OUT], BF16, name="ctr_w")
        nc.scalar.dma_start(ctr_w[:], w_ctr)
        gain_col = held.tile([P, HALVES], F32, name="gain_col")
        bias_col = held.tile([P, HALVES], F32, name="bias_col")
        with nc.allow_non_contiguous_dma(reason="one float32 to a partition, 256 in all"):
            nc.sync.dma_start(gain_col[:], gain.rearrange("(h p) o -> p (h o)", p=P))
            nc.scalar.dma_start(bias_col[:], bias.rearrange("(h p) o -> p (h o)", p=P))

        neg_points = held.tile([P, POINTS], BF16, name="neg_points")
        nc.vector.tensor_scalar_mul(neg_points[:], points[:], -1.0)
        neg_gain_col = held.tile([P, HALVES], F32, name="neg_gain_col")
        nc.vector.tensor_scalar_mul(neg_gain_col[:], gain_col[:], -1.0)
        eps_col = held.tile([P, 1], F32, name="eps_col")
        nc.vector.memset(eps_col[:], EPS)
        table_warmer = held.tile([P, 1], F32, name="table_warmer")
        nc.scalar.activation(table_warmer[:], eps_col[:], ACT.Abs_reciprocal_sqrt)

        point_parts = [slice(0, POINTS // 2), slice(POINTS // 2, POINTS)]
        halves = [slice(h * P, (h + 1) * P) for h in range(HALVES)]
        pieces = [offsets[:, r * (POINTS // 16) : (r + 1) * (POINTS // 16)] for r in range(NEIGHBOURS)]
        y = [[psum.tile([P, POINTS], F32, name=f"y{h}_{r}") for r in range(NEIGHBOURS)] for h in range(HALVES)]
        for i in range(WARM_MATMULS):
            nc.tensor.matmul(y[HALVES - 1][NEIGHBOURS - 1][:], zeros[:, 0:P], zeros[:], start=True, stop=True)
        for r in range(NEIGHBOURS):
            nc.tensor.matmul(y[0][r][:], nbr_w[:, halves[0]], points[:].indirect(pieces[r]), start=True, stop=False)
        for r in range(NEIGHBOURS):
            nc.tensor.matmul(y[0][r][:], ctr_w[:, halves[0]], points[:], start=False, stop=False)
            nc.tensor.matmul(y[0][r][:], nbr_w[:, halves[0]], neg_points[:], start=False, stop=True)
        for r in range(NEIGHBOURS):
            for i, t in enumerate(point_parts):
                nc.tensor.matmul(y[1][r][:, t], ctr_w[:, halves[1]], points[:, t], start=i == 0, stop=False)
            for t in point_parts:
                nc.tensor.matmul(y[1][r][:, t], nbr_w[:, halves[1]], neg_points[:, t], start=False, stop=False)
        for r in range(NEIGHBOURS):
            nc.tensor.matmul(y[1][r][:], nbr_w[:, halves[1]], points[:].indirect(pieces[r]), start=False, stop=True)

        z = [[work.tile([P, POINTS], F32, name="z") for r in range(NEIGHBOURS)] for h in range(HALVES)]

        def parts(h, r):
            return point_parts if (h, r) == (HALVES - 1, NEIGHBOURS - 1) else [slice(0, POINTS)]

        for h in range(HALVES):
            stats = small.tile([P, NEIGHBOURS, STATS], F32, name="stats")
            for r in range(NEIGHBOURS):
                nc.vector.bn_stats(stats[:, r, :], y[h][r][:])
            mean_var = small.tile([P, 2], F32, name="mean_var")
            nc.vector.bn_aggr(mean_var[:], stats[:].rearrange("p r s -> p (r s)"))
            rstd = small.tile([P, 1], F32, name="rstd")
            nc.scalar.activation(rstd[:], mean_var[:, 1:2], ACT.Abs_reciprocal_sqrt, bias=eps_col[:], scale=1.0)
            neg_mean_gain = small.tile([P, 1], F32, name="neg_mean_gain")
            nc.scalar.activation(neg_mean_gain[:], mean_var[:, 0:1], ACT.Identity, scale=neg_gain_col[:, h : h + 1])
            scale = small.tile([P, 1], F32, name="scale")
            nc.scalar.activation(scale[:], rstd[:], ACT.Identity, scale=gain_col[:, h : h + 1])
            shift = small.tile([P, 1], F32, name="shift")
            nc.scalar.activation(shift[:], rstd[:], ACT.Identity, bias=bias_col[:, h : h + 1], scale=neg_mean_gain[:])
            for r in range(NEIGHBOURS):
                if h == HALVES - 1 and r == 0:
                    centred = work.tile([P, POINTS], F32, name="centred")
                    nc.vector.tensor_scalar(
                        centred[:], y[h][r][:], mean_var[:, 0:1], gain_col[:, h : h + 1], ALU.subtract, ALU.mult
                    )
                    nc.scalar.activation(
                        z[h][r][:], centred[:], ACT.Identity, bias=bias_col[:, h : h + 1], scale=rstd[:]
                    )
                else:
                    for t in parts(h, r):
                        nc.scalar.activation(z[h][r][:, t], y[h][r][:, t], ACT.Identity, bias=shift[:], scale=scale[:])

        for h in range(HALVES):
            for r in range(NEIGHBOURS):
                for t in parts(h, r):
                    z_part = z[h][r][:, t]
                    result = work.tile([P, t.stop - t.start], F32, name=f"result{t.start}_{t.stop}")
                    nc.vector.scalar_tensor_tensor(result[:], z_part, SLOPE, z_part, ALU.mult, ALU.max)
                    nc.sync.dma_start(out[halves[h], r * POINTS + t.start : r * POINTS + t.stop], result[:])
